import numpy as np
import ml_dtypes


def mxq(x, axis, fmt="e4m3"):
    dtype, down = {"e4m3": (ml_dtypes.float8_e4m3fn, 7), "e5m2": (ml_dtypes.float8_e5m2, 14)}[fmt]
    v = np.moveaxis(np.asarray(x, np.float32).astype(ml_dtypes.bfloat16).astype(np.float64), axis, -1)
    blocks = v.reshape(v.shape[:-1] + (-1, 32))
    amax = np.abs(blocks).max(-1, keepdims=True)
    byte = np.maximum(np.where(amax > 0, np.frexp(amax)[1] - 1 + 127, 0) - down, 1)
    scale = np.exp2(byte - 127.0)
    codes = (blocks / scale).astype(np.float32).astype(dtype).astype(np.float64)
    return np.moveaxis((codes * scale).reshape(v.shape), -1, axis)


WIDE = False


def mx_kscale(k):
    if not WIDE:
        return np.ones(k)
    levels = np.array([18, -18])
    if k % 512:
        return np.exp2(np.random.permutation(np.resize(levels, k // 32))).repeat(32)
    a = np.empty((k // 512, 16))
    for p in range(k // 512):
        a[p, :8] = np.random.permutation(np.resize(levels, 8))
        for g in range(8):
            far = levels[np.abs(levels - a[p, g]) >= 10]
            a[p, g + 8] = far[np.random.randint(len(far))]
    return np.exp2(a.ravel()).repeat(32)


BF16 = ml_dtypes.bfloat16


def bf(x):
    return np.asarray(x, np.float32).astype(BF16)


def f64(x):
    return np.asarray(x).astype(np.float64)


B, CIN, HID, COUT, H, W = 1, 512, 1024, 512, 16, 32
P = H * W
EXTRA = 64


def parts(p, m, n):
    return p[:m, :n] + p[m:, n:], p[:m, n:] - p[m:, :n]


def setup_inputs():
    s = mx_kscale(P)
    u = mx_kscale(COUT)
    v = mx_kscale(HID)
    sg = s.reshape(1, 1, H, W, 1)
    xa = bf(np.random.standard_normal((B, CIN, P + EXTRA, 2)))
    w0_0 = bf(np.random.standard_normal((CIN, HID, 2)) * 0.7 / np.sqrt(CIN))
    wout_0 = bf(np.random.standard_normal((HID, COUT, 2)) * 0.8 / np.sqrt(HID))
    xf, wf = f64(xa), f64(w0_0)
    za = wf[..., 0].T @ xf[0, :, :, 0] - wf[..., 1].T @ xf[0, :, :, 1]
    keep = np.sort(np.argsort(np.min(np.abs(za), axis=0))[EXTRA:])
    x0 = xa[:, :, keep, :].reshape(B, CIN, H, W, 2)
    xk = f64(x0).reshape(CIN, P, 2)
    zr = (wf[..., 0].T @ xk[..., 0] - wf[..., 1].T @ xk[..., 1]).reshape(B, HID, H, W)
    g = bf(np.random.standard_normal((B, COUT, H, W, 2)) * np.exp2(np.random.randint(-6, 1, (1, 1, H, W, 1))) / sg * u[None, :, None, None, None])
    return {"x": bf(f64(x0) * sg),
            "w0": bf(f64(w0_0) / v[None, :, None]),
            "wout": bf(f64(wout_0) * v[:, None, None] / u[None, :, None]),
            "zr": np.asarray(zr, np.float32),
            "grad_out": g}


def reference(x, w0, wout, zr, grad_out):
    g = f64(grad_out).reshape(COUT, P, 2).transpose(0, 2, 1).reshape(COUT, 2 * P)
    wo = f64(wout).transpose(2, 0, 1).reshape(2 * HID, COUT)
    w = f64(w0).transpose(2, 0, 1).reshape(2 * CIN, HID)
    xt = f64(x).reshape(CIN, P, 2).transpose(2, 0, 1).reshape(2 * CIN, P)
    ph = mxq(wo, 1, "e4m3") @ mxq(g, 0, "e5m2")
    dhr, dhi = parts(ph, HID, P)
    dzr = dhr * (f64(zr).reshape(HID, P) > 0.0)
    dzi = dhi
    px = mxq(w, 1, "e4m3") @ mxq(np.concatenate([dzr, dzi], axis=1), 0, "e5m2")
    dxr, dxi = parts(px, CIN, P)
    pw = mxq(xt, 1, "e4m3") @ mxq(np.concatenate([dzr, dzi], axis=0), 1, "e5m2").T
    dwr, dwi = parts(pw, CIN, HID)
    dx = np.stack([dxr.reshape(B, CIN, H, W), dxi.reshape(B, CIN, H, W)], axis=-1)
    dw0 = np.stack([dwr, dwi], axis=-1)
    return dx, dw0

@@ -1,0 +1,395 @@
+from contextlib import ExitStack
+
+import concourse.mybir as mybir
+from concourse.masks import make_identity
+
+F32 = mybir.dt.float32
+BF16 = mybir.dt.bfloat16
+U32 = mybir.dt.uint32
+U8 = mybir.dt.uint8
+E4M3 = mybir.dt.float8_e4m3fn_x4
+E5M2 = mybir.dt.float8_e5m2_x4
+ALU = mybir.AluOpType
+
+P = 128
+CIN, HID, COUT, TOK = 512, 1024, 512, 512
+NTP = 3
+NVALS = 4
+NRES = 6
+FLOPS = 3 * 4 * 2 * 512 * 512 * 1024
+
+
+def tile_spectralattention_v_kernel(tc, x, w0, wout, zr, grad_out, out_0, out_1):
+    nc = tc.nc
+    with ExitStack() as ctx:
+        keep = ctx.enter_context(tc.tile_pool(name="keep", bufs=1))
+        work = ctx.enter_context(tc.tile_pool(name="work", bufs=2))
+        psum = ctx.enter_context(tc.psum_pool(name="psum", bufs=1))
+        ctx.enter_context(tc.manual_schedule())
+
+        def copy(eng, out, in_):
+            if eng == "V":
+                nc.vector.tensor_copy(out=out, in_=in_)
+            else:
+                nc.scalar.copy(out=out, in_=in_)
+
+        def load(name, src, dtype):
+            width = src.shape[1] if len(src.shape) == 2 else src.shape[1] * src.shape[2]
+            dst = keep.tile([P, width], dtype, name=name)
+            view = dst[:]
+            if len(src.shape) == 3:
+                view = view.rearrange("p (a w) -> p a w", a=src.shape[1])
+            nc.sync.dma_start(out=view, in_=src)
+            return dst
+
+        def operand(name, width):
+            codes = keep.tile([P, width], U32, name=name + "_codes", align_bytes=64)
+            scales = keep.tile([P, width], U8, name=name + "_scales", align_bytes=64)
+            return codes, scales
+
+        def quantize(op, fmt, first, values):
+            width = values.shape[1] // 4
+            cols = slice(first, first + width)
+            nc.vector.quantize_mx(out=op[0][:, cols].bitcast(fmt), scales=op[1][:, cols], in_=values)
+
+        def mx(bank, weights, w_first, moving, m_first, start, stop):
+            w_cols = slice(w_first, w_first + P)
+            m_cols = slice(m_first, m_first + 512)
+            nc.tensor.matmul_mx(
+                out=bank[:],
+                lhsT=weights[0][:, w_cols].bitcast(E4M3),
+                lhsT_scale=weights[1][:, w_cols],
+                rhs=moving[0][:, m_cols].bitcast(E5M2),
+                rhs_scale=moving[1][:, m_cols],
+                start=start,
+                stop=stop,
+            )
+
+        turns = {"tp": 0, "acc": 0}
+
+        def bank_at(n):
+            bank = psum.tile([P, 512], F32, name="bank%d" % n, tag="bank%d" % n)
+            return bank
+
+        def tp_bank():
+            turns["tp"] = turns["tp"] + 1
+            return bank_at((turns["tp"] - 1) % NTP)
+
+        def acc_bank():
+            turns["acc"] = turns["acc"] + 1
+            return bank_at(NTP + (turns["acc"] - 1) % (8 - NTP))
+
+        def negate(out, in_):
+            nc.vector.tensor_scalar(out=out, in0=in_, scalar1=-1.0, scalar2=None, op0=ALU.mult)
+
+        ident = keep.tile([P, P], F32, name="ident")
+        make_identity(nc, ident[:])
+
+        wout_v = wout.rearrange("(g m t) o c -> g m t (o c)", g=2, t=4)
+        zr_v = zr.rearrange("b (g m t) y z -> (b g) m t (y z)", g=2, t=4)
+        g_v = grad_out.rearrange("b (q t) y z c -> (b q) t (y z c)", t=4)
+        x_v = x.rearrange("b (a m) y z c -> m (b a) (y z c)", m=P)
+        w0_v = w0.rearrange("(a m) h c -> a m (h c)", m=P)
+        dx_v = out_0.rearrange("b i y z c -> (b i) (y z c)")
+        dw_v = out_1.rearrange("i h c -> i (h c)")
+
+        S = {}
+
+        g_vals = work.tile([P, 6144], BF16, name="g_vals", tag="vals", bufs=NVALS, align_bytes=64)
+        g_op = operand("g", 1536)
+
+        def g_sort(eng, half, lo=0, hi=2):
+            dst = g_vals[:, 0:4096].rearrange("p (c h y i t) -> p h c y t i", c=2, h=2, i=4, t=4)[:, half]
+            src = S["g", half][:].rearrange("p (t y i c) -> p c y t i", t=4, i=4, c=2)
+            copy(eng, dst[:, lo:hi], src[:, lo:hi])
+
+        def direct_turn(t):
+            words = S["wout0", t][:].bitcast(F32)
+            bank = tp_bank()
+            for s in range(4):
+                nc.tensor.transpose(bank[:, s * P : (s + 1) * P], words[:, s:512:4], ident[:])
+            S["dbank", t] = bank
+
+        def direct_out(t):
+            vals = work.tile([P, 1024], BF16, name="dvals", tag="dvals", bufs=3, align_bytes=64)
+            nc.scalar.copy(
+                out=vals[:].rearrange("p (c m s) -> p c m s", c=2, s=4),
+                in_=S["dbank", t][:].bitcast(BF16).rearrange("p (s m c) -> p c m s", s=4, c=2),
+            )
+            S["dvals", t] = vals
+
+        def direct_quant(t):
+            op = operand("wd%d" % t, 256)
+            quantize(op, E4M3, 0, S["dvals", t][:])
+            S["wop", 0, t] = (op, 0, P)
+
+        def unit_sort(eng, key, src, tokens):
+            pre = work.tile([P, 2048], BF16, name="pre", tag="pre", bufs=2)
+            if tokens:
+                a = src.rearrange("p (b u j c) -> p c u b j", u=2, j=16, c=2)
+                o = pre[:].rearrange("p (c u b j) -> p c u b j", c=2, u=2, j=16)
+            else:
+                a = src.rearrange("p (q u e c) -> p c u q e", u=2, e=2, c=2)
+                o = pre[:].rearrange("p (c u q e) -> p c u q e", c=2, u=2, e=2)
+            copy(eng, o, a)
+            S["pre", key] = pre
+
+        def unit_turn(key, c):
+            bank = tp_bank()
+            for s in range(4):
+                first = c * 1024 + s * 256
+                nc.tensor.transpose(
+                    bank[:, s * P : (s + 1) * P], S["pre", key][:, first : first + 256].bitcast(F32), ident[:]
+                )
+            S["ubank", key, c] = bank
+
+        def unit_out(eng, key, c):
+            if c == 0:
+                vals = work.tile([P, 2048], BF16, name="uvals", tag="uvals", bufs=2, align_bytes=64)
+                S["uvals", key] = vals
+            dst = S["uvals", key][:, c * 1024 : (c + 1) * 1024].bitcast(F32).rearrange("p (m u) -> p m u", u=2)
+            copy(eng, dst, S["ubank", key, c][:].rearrange("p (u m) -> p m u", u=2))
+
+        def unit_quant(key):
+            op = operand("u_%s%d" % key, 512)
+            quantize(op, E4M3, 0, S["uvals", key][:])
+            S["uop", key] = op
+
+        def dh(g, t, parts=(0, 1)):
+            if g == 0:
+                op, r_first, i_first = S["wop", 0, t]
+            else:
+                op, r_first, i_first = S["uop", ("w", t // 2)], (t % 2) * P, 256 + (t % 2) * P
+            for c in parts:
+                bank = acc_bank()
+                mx(bank, op, r_first, g_op, 512 * c, True, False)
+                mx(bank, op, i_first, g_op, 512 * (c + 1), False, True)
+                S["dh", g, t, c] = bank
+
+        def dz_tile(g):
+            if ("dz", g) not in S:
+                dz = keep.tile([P, 4096], BF16, name="dz%d" % g)
+                S["dz", g] = dz
+            return S["dz", g]
+
+        def dz_re(g, t):
+            saved = S["zr", g, t // 2][:, (t % 2) * 512 : (t % 2 + 1) * 512]
+            saved = saved.rearrange("p (b u j) -> p u b j", u=2, j=16)
+            bank = S["dh", g, t, 0][:].rearrange("p (b u j) -> p u b j", u=2, j=16)
+            dst = dz_tile(g)[:, t * 1024 : t * 1024 + 512].rearrange("p (u b j) -> p u b j", u=2, j=16)
+            for u in range(2):
+                nc.vector.scalar_tensor_tensor(
+                    out=dst[:, u], in0=saved[:, u], scalar=0.0, in1=bank[:, u], op0=ALU.is_gt, op1=ALU.mult
+                )
+
+        def dz_im(eng, g, t):
+            dst = dz_tile(g)[:, t * 1024 + 512 : (t + 1) * 1024].rearrange("p (u b j) -> p b u j", u=2, j=16)
+            copy(eng, dst, S["dh", g, t, 1][:].rearrange("p (b u j) -> p b u j", u=2, j=16))
+
+        def tok_turn(g, a, c):
+            bank = tp_bank()
+            for s in range(4):
+                first = (2 * a + s // 2) * 1024 + c * 512 + (s % 2) * 256
+                nc.tensor.transpose(
+                    bank[:, s * P : (s + 1) * P], S["dz", g][:, first : first + 256].bitcast(F32), ident[:]
+                )
+            S["tbank", g, a, c] = bank
+
+        def vals_tile(kind, g):
+            if (kind, g) not in S:
+                vals = work.tile([P, 6144], BF16, name=kind, tag="vals", bufs=NVALS, align_bytes=64)
+                S[kind, g] = vals
+                S[kind + "op", g] = operand("%s%d" % (kind, g), 1536)
+            return S[kind, g]
+
+        def tok_out(eng, g, a, c):
+            dst = vals_tile("tok", g)[:].bitcast(F32).rearrange("p (k c m a s) -> p c a k m s", k=2, c=3, a=2, s=4)
+            copy(eng, dst[:, c, a], S["tbank", g, a, c][:].rearrange("p (s k m) -> p k m s", s=4, k=2))
+
+        def hid_sort(eng, g, k, lo=0, hi=4):
+            dst = vals_tile("hid", g)[:, k * 3072 : k * 3072 + 2048].rearrange("p (v y i t) -> p v y t i", v=4, i=4, t=4)
+            src = S["dz", g][:].rearrange("p (t v k y i) -> p k v y t i", t=4, v=4, k=2, i=4)[:, k]
+            copy(eng, dst[:, lo:hi], src[:, lo:hi])
+
+        def neg(kind, g, k):
+            vals = S[kind, g]
+            negate(vals[:, k * 3072 + 2048 : (k + 1) * 3072], vals[:, k * 3072 : k * 3072 + 1024])
+
+        def quant_a(kind, g, k):
+            quantize(S[kind + "op", g], E5M2, k * 768, S[kind, g][:, k * 3072 : k * 3072 + 2048])
+
+        def quant_b(kind, g, k):
+            quantize(S[kind + "op", g], E5M2, k * 768 + 512, S[kind, g][:, k * 3072 + 2048 : (k + 1) * 3072])
+
+        def dw(g, k, it):
+            op, first = S["uop", ("x", it // 2)], (it % 2) * P
+            bank = acc_bank()
+            mx(bank, op, first, S["tokop", g], k * 768, True, False)
+            mx(bank, op, 256 + first, S["tokop", g], k * 768 + 256, False, True)
+            S["dw", g, k, it] = bank
+
+        def dw_out(eng, g, k, it):
+            res = work.tile([P, 512], F32, name="res", tag="res", bufs=NRES)
+            copy(eng, res[:].rearrange("p (h c) -> p h c", c=2), S["dw", g, k, it][:].rearrange("p (c h) -> p h c", c=2))
+            first = g * 1024 + k * 512
+            nc.sync.dma_start(out=dw_v[it * P : (it + 1) * P, first : first + 512], in_=res[:])
+
+        def dx(k, it, g, n=None):
+            op = S["uop", ("i", it)]
+            if g == 0:
+                S["dx", k, it] = acc_bank() if n is None else bank_at(n)
+            bank = S["dx", k, it]
+            mx(bank, op, g * P, S["hidop", g], k * 768, g == 0, False)
+            mx(bank, op, 256 + g * P, S["hidop", g], k * 768 + 256, False, g == 1)
+
+        def dx_out(eng, k, it):
+            res = work.tile([P, 512], F32, name="res", tag="res", bufs=NRES)
+            copy(
+                eng,
+                res[:].rearrange("p (b u j c) -> p b u j c", u=2, j=16, c=2),
+                S["dx", k, it][:].rearrange("p (c u b j) -> p b u j c", c=2, u=2, j=16),
+            )
+            nc.sync.dma_start(out=dx_v[it * P : (it + 1) * P, k * 512 : (k + 1) * 512], in_=res[:])
+
+
+        def unit_pe(key, eng="S"):
+            for c in range(2):
+                unit_turn(key, c)
+                unit_out(eng, key, c)
+
+        def sort(key, eng="V"):
+            unit_sort(eng, key, S[key][:], key[0] == "x")
+
+        def tok_pe(g, a):
+            for c in range(2):
+                tok_turn(g, a, c)
+                tok_out("S", g, a, c)
+
+        def dz(g, t):
+            dz_re(g, t)
+            dz_im("S", g, t)
+
+        def dw4(g, k, engs="SSSS"):
+            for it in range(4):
+                dw(g, k, it)
+                dw_out(engs[it], g, k, it)
+
+        S["wout0", 0] = load("wout00", wout_v[0, :, 0, :], BF16)
+        S["g", 0] = load("g0", g_v[:, :, 0:512], BF16)
+        S["g", 1] = load("g1", g_v[:, :, 512:1024], BF16)
+        for t in range(1, 4):
+            S["wout0", t] = load("wout0%d" % t, wout_v[0, :, t, :], BF16)
+        S["w", 0] = load("wout10", wout_v[1, :, 0:2, :], BF16)
+        S["zr", 0, 0] = load("zr00", zr_v[0, :, 0:2, :], F32)
+        S["w", 1] = load("wout11", wout_v[1, :, 2:4, :], BF16)
+        S["zr", 0, 1] = load("zr01", zr_v[0, :, 2:4, :], F32)
+        S["x", 0] = load("x0", x_v[:, 0:2, :], BF16)
+        S["zr", 1, 0] = load("zr10", zr_v[1, :, 0:2, :], F32)
+        S["x", 1] = load("x1", x_v[:, 2:4, :], BF16)
+        S["zr", 1, 1] = load("zr11", zr_v[1, :, 2:4, :], F32)
+        for it in range(4):
+            S["i", it] = load("w0%d" % it, w0_v[it], BF16)
+
+        direct_turn(0)
+        direct_out(0)
+        g_sort("V", 0)
+        g_sort("V", 1, 0, 1)
+        g_sort("S", 1, 1, 2)
+        for t in range(1, 4):
+            direct_turn(t)
+            direct_out(t)
+            if t == 1:
+                quantize(g_op, E5M2, 0, g_vals[:, 0:2048])
+                direct_quant(0)
+                quantize(g_op, E5M2, 512, g_vals[:, 2048:4096])
+                negate(g_vals[:, 4096:6144], g_vals[:, 0:2048])
+                direct_quant(1)
+                quantize(g_op, E5M2, 1024, g_vals[:, 4096:6144])
+        sort(("w", 0))
+        dh(0, 0)
+        direct_quant(2)
+        dh(0, 1)
+        direct_quant(3)
+        dz(0, 0)
+        unit_pe(("w", 0))
+        sort(("w", 1))
+        dh(0, 2)
+        dz(0, 1)
+        unit_quant(("w", 0))
+        dh(0, 3)
+        dz(0, 2)
+        unit_pe(("w", 1))
+        sort(("x", 0))
+        dz(0, 3)
+        dh(1, 0)
+        unit_quant(("w", 1))
+        tok_pe(0, 0)
+        unit_pe(("x", 0))
+        sort(("x", 1))
+        dh(1, 1)
+        dz(1, 0)
+        tok_pe(0, 1)
+        unit_quant(("x", 0))
+        dh(1, 2)
+        dz(1, 1)
+        unit_pe(("x", 1))
+        neg("tok", 0, 0)
+        dh(1, 3)
+        dz(1, 2)
+        quant_a("tok", 0, 0)
+        quant_b("tok", 0, 0)
+        unit_quant(("x", 1))
+        neg("tok", 0, 1)
+        dz(1, 3)
+        quant_a("tok", 0, 1)
+        quant_b("tok", 0, 1)
+        sort(("i", 0))
+        tok_pe(1, 0)
+        dw4(0, 0)
+        sort(("i", 1))
+        tok_pe(1, 1)
+        unit_pe(("i", 0))
+        hid_sort("V", 0, 0)
+        dw4(0, 1)
+        unit_quant(("i", 0))
+        neg("tok", 1, 0)
+        neg("hid", 0, 0)
+        quant_a("tok", 1, 0)
+        quant_b("tok", 1, 0)
+        sort(("i", 2))
+        unit_pe(("i", 1))
+        quant_a("hid", 0, 0)
+        quant_b("hid", 0, 0)
+        neg("tok", 1, 1)
+        dw4(1, 0)
+        sort(("i", 3))
+        unit_quant(("i", 1))
+        quant_a("tok", 1, 1)
+        quant_b("tok", 1, 1)
+        unit_pe(("i", 2))
+        hid_sort("V", 0, 1)
+        unit_pe(("i", 3))
+        unit_quant(("i", 2))
+        neg("hid", 0, 1)
+        hid_sort("V", 1, 0)
+        unit_quant(("i", 3))
+        quant_a("hid", 0, 1)
+        quant_b("hid", 0, 1)
+        dw4(1, 1)
+        neg("hid", 1, 0)
+        for it in range(4):
+            dx(0, it, 0, it)
+        hid_sort("V", 1, 1)
+        quant_a("hid", 1, 0)
+        quant_b("hid", 1, 0)
+        neg("hid", 1, 1)
+        for it in range(4):
+            dx(1, it, 0, 4 + it)
+        quant_a("hid", 1, 1)
+        quant_b("hid", 1, 1)
+        for it in range(4):
+            dx(0, it, 1)
+            dx_out("SVSV"[it], 0, it)
+        for it in range(4):
+            dx(1, it, 1)
+            dx_out("SVSV"[it], 1, it)

@@ -13,9 +13,11 @@ ALU = mybir.AluOpType
 
 P = 128
 CIN, HID, COUT, TOK = 512, 1024, 512, 512
-NTP = 3
+NTP = 4
 NVALS = 4
-NRES = 6
+NRES = 8
+NPRE = 3
+NUV = 3
 FLOPS = 3 * 4 * 2 * 512 * 512 * 1024
 
 
@@ -111,7 +113,7 @@ def tile_spectralattention_v_kernel(tc, x, w0, wout, zr, grad_out, out_0, out_1)
             S["dbank", t] = bank
 
         def direct_out(t):
-            vals = work.tile([P, 1024], BF16, name="dvals", tag="dvals", bufs=3, align_bytes=64)
+            vals = work.tile([P, 1024], BF16, name="dvals", tag="dvals", bufs=2, align_bytes=64)
             nc.scalar.copy(
                 out=vals[:].rearrange("p (c m s) -> p c m s", c=2, s=4),
                 in_=S["dbank", t][:].bitcast(BF16).rearrange("p (s m c) -> p c m s", s=4, c=2),
@@ -123,15 +125,19 @@ def tile_spectralattention_v_kernel(tc, x, w0, wout, zr, grad_out, out_0, out_1)
             quantize(op, E4M3, 0, S["dvals", t][:])
             S["wop", 0, t] = (op, 0, P)
 
-        def unit_sort(eng, key, src, tokens):
-            pre = work.tile([P, 2048], BF16, name="pre", tag="pre", bufs=2)
+        def unit_sort(engs, key, src, tokens):
+            pre = work.tile([P, 2048], BF16, name="pre", tag="pre", bufs=NPRE)
             if tokens:
                 a = src.rearrange("p (b u j c) -> p c u b j", u=2, j=16, c=2)
                 o = pre[:].rearrange("p (c u b j) -> p c u b j", c=2, u=2, j=16)
             else:
                 a = src.rearrange("p (q u e c) -> p c u q e", u=2, e=2, c=2)
                 o = pre[:].rearrange("p (c u q e) -> p c u q e", c=2, u=2, e=2)
-            copy(eng, o, a)
+            if len(engs) == 2:
+                for c in range(2):
+                    copy(engs[c], o[:, c], a[:, c])
+            else:
+                copy(engs, o, a)
             S["pre", key] = pre
 
         def unit_turn(key, c):
@@ -145,7 +151,7 @@ def tile_spectralattention_v_kernel(tc, x, w0, wout, zr, grad_out, out_0, out_1)
 
         def unit_out(eng, key, c):
             if c == 0:
-                vals = work.tile([P, 2048], BF16, name="uvals", tag="uvals", bufs=2, align_bytes=64)
+                vals = work.tile([P, 2048], BF16, name="uvals", tag="uvals", bufs=NUV, align_bytes=64)
                 S["uvals", key] = vals
             dst = S["uvals", key][:, c * 1024 : (c + 1) * 1024].bitcast(F32).rearrange("p (m u) -> p m u", u=2)
             copy(eng, dst, S["ubank", key, c][:].rearrange("p (u m) -> p m u", u=2))
@@ -156,10 +162,10 @@ def tile_spectralattention_v_kernel(tc, x, w0, wout, zr, grad_out, out_0, out_1)
             S["uop", key] = op
 
         def dh(g, t, parts=(0, 1)):
-            if g == 0:
-                op, r_first, i_first = S["wop", 0, t]
+            if ("wop", g, t) in S:
+                op, r_first, i_first = S["wop", g, t]
             else:
-                op, r_first, i_first = S["uop", ("w", t // 2)], (t % 2) * P, 256 + (t % 2) * P
+                op, r_first, i_first = S["uop", ("vw"[g], t // 2)], (t % 2) * P, 256 + (t % 2) * P
             for c in parts:
                 bank = acc_bank()
                 mx(bank, op, r_first, g_op, 512 * c, True, False)
@@ -252,18 +258,18 @@ def tile_spectralattention_v_kernel(tc, x, w0, wout, zr, grad_out, out_0, out_1)
             nc.sync.dma_start(out=dx_v[it * P : (it + 1) * P, k * 512 : (k + 1) * 512], in_=res[:])
 
 
-        def unit_pe(key, eng="S"):
+        def unit_pe(key, engs="SS"):
             for c in range(2):
                 unit_turn(key, c)
-                unit_out(eng, key, c)
+                unit_out(engs[c], key, c)
 
-        def sort(key, eng="V"):
-            unit_sort(eng, key, S[key][:], key[0] == "x")
+        def sort(key, engs="V"):
+            unit_sort(engs, key, S[key][:], key[0] == "x")
 
-        def tok_pe(g, a):
+        def tok_pe(g, a, engs="SS"):
             for c in range(2):
                 tok_turn(g, a, c)
-                tok_out("S", g, a, c)
+                tok_out(engs[c], g, a, c)
 
         def dz(g, t):
             dz_re(g, t)
@@ -274,15 +280,19 @@ def tile_spectralattention_v_kernel(tc, x, w0, wout, zr, grad_out, out_0, out_1)
                 dw(g, k, it)
                 dw_out(engs[it], g, k, it)
 
-        S["wout0", 0] = load("wout00", wout_v[0, :, 0, :], BF16)
+        def quant(kind, g, k):
+            quant_a(kind, g, k)
+            quant_b(kind, g, k)
+
+        S["v", 0] = load("wout00", wout_v[0, :, 0:2, :], BF16)
         S["g", 0] = load("g0", g_v[:, :, 0:512], BF16)
         S["g", 1] = load("g1", g_v[:, :, 512:1024], BF16)
-        for t in range(1, 4):
+        for t in range(2, 4):
             S["wout0", t] = load("wout0%d" % t, wout_v[0, :, t, :], BF16)
-        S["w", 0] = load("wout10", wout_v[1, :, 0:2, :], BF16)
         S["zr", 0, 0] = load("zr00", zr_v[0, :, 0:2, :], F32)
-        S["w", 1] = load("wout11", wout_v[1, :, 2:4, :], BF16)
+        S["w", 0] = load("wout10", wout_v[1, :, 0:2, :], BF16)
         S["zr", 0, 1] = load("zr01", zr_v[0, :, 2:4, :], F32)
+        S["w", 1] = load("wout11", wout_v[1, :, 2:4, :], BF16)
         S["x", 0] = load("x0", x_v[:, 0:2, :], BF16)
         S["zr", 1, 0] = load("zr10", zr_v[1, :, 0:2, :], F32)
         S["x", 1] = load("x1", x_v[:, 2:4, :], BF16)
@@ -290,106 +300,105 @@ def tile_spectralattention_v_kernel(tc, x, w0, wout, zr, grad_out, out_0, out_1)
         for it in range(4):
             S["i", it] = load("w0%d" % it, w0_v[it], BF16)
 
-        direct_turn(0)
-        direct_out(0)
+        sort(("v", 0), "VV")
+        unit_pe(("v", 0))
         g_sort("V", 0)
         g_sort("V", 1, 0, 1)
         g_sort("S", 1, 1, 2)
-        for t in range(1, 4):
+        for t in range(2, 4):
             direct_turn(t)
             direct_out(t)
-            if t == 1:
-                quantize(g_op, E5M2, 0, g_vals[:, 0:2048])
-                direct_quant(0)
-                quantize(g_op, E5M2, 512, g_vals[:, 2048:4096])
-                negate(g_vals[:, 4096:6144], g_vals[:, 0:2048])
-                direct_quant(1)
-                quantize(g_op, E5M2, 1024, g_vals[:, 4096:6144])
-        sort(("w", 0))
-        dh(0, 0)
+        quantize(g_op, E5M2, 0, g_vals[:, 0:2048])
+        unit_quant(("v", 0))
+        quantize(g_op, E5M2, 512, g_vals[:, 2048:4096])
+        negate(g_vals[:, 4096:6144], g_vals[:, 0:2048])
         direct_quant(2)
+        quantize(g_op, E5M2, 1024, g_vals[:, 4096:6144])
+
+        def dw_run(pairs, engs):
+            for n, (g, k, it) in enumerate(pairs):
+                dw(g, k, it)
+                dw_out(engs[n], g, k, it)
+
+        def full(kind, g, k):
+            neg(kind, g, k)
+            quant(kind, g, k)
+
+        sort(("w", 0), "VS")
+        dh(0, 0)
         dh(0, 1)
         direct_quant(3)
         dz(0, 0)
+        dz(0, 1)
         unit_pe(("w", 0))
         sort(("w", 1))
         dh(0, 2)
-        dz(0, 1)
-        unit_quant(("w", 0))
         dh(0, 3)
-        dz(0, 2)
-        unit_pe(("w", 1))
         sort(("x", 0))
+        unit_quant(("w", 0))
+        dz(0, 2)
         dz(0, 3)
-        dh(1, 0)
-        unit_quant(("w", 1))
-        tok_pe(0, 0)
+        unit_pe(("w", 1))
         unit_pe(("x", 0))
         sort(("x", 1))
+        dh(1, 0)
         dh(1, 1)
+        unit_quant(("w", 1))
         dz(1, 0)
+        dz(1, 1)
+        tok_pe(0, 0)
         tok_pe(0, 1)
+        sort(("i", 0))
         unit_quant(("x", 0))
         dh(1, 2)
-        dz(1, 1)
-        unit_pe(("x", 1))
-        neg("tok", 0, 0)
         dh(1, 3)
         dz(1, 2)
-        quant_a("tok", 0, 0)
-        quant_b("tok", 0, 0)
-        unit_quant(("x", 1))
+        neg("tok", 0, 0)
         neg("tok", 0, 1)
+        quant("tok", 0, 0)
         dz(1, 3)
-        quant_a("tok", 0, 1)
-        quant_b("tok", 0, 1)
-        sort(("i", 0))
-        tok_pe(1, 0)
-        dw4(0, 0)
-        sort(("i", 1))
-        tok_pe(1, 1)
+        quant("tok", 0, 1)
+        unit_pe(("x", 1))
         unit_pe(("i", 0))
-        hid_sort("V", 0, 0)
-        dw4(0, 1)
-        unit_quant(("i", 0))
-        neg("tok", 1, 0)
-        neg("hid", 0, 0)
-        quant_a("tok", 1, 0)
-        quant_b("tok", 1, 0)
+        sort(("i", 1))
+        unit_quant(("x", 1))
+        dw_run([(0, 0, 0), (0, 0, 1), (0, 1, 0), (0, 1, 1)], "SSSV")
+        tok_pe(1, 0)
+        tok_pe(1, 1)
         sort(("i", 2))
+        unit_quant(("i", 0))
+        hid_sort("V", 0, 0)
+        dw_run([(0, 0, 2), (0, 0, 3), (0, 1, 2), (0, 1, 3)], "SSSV")
+        full("tok", 1, 0)
         unit_pe(("i", 1))
-        quant_a("hid", 0, 0)
-        quant_b("hid", 0, 0)
-        neg("tok", 1, 1)
-        dw4(1, 0)
-        sort(("i", 3))
-        unit_quant(("i", 1))
-        quant_a("tok", 1, 1)
-        quant_b("tok", 1, 1)
         unit_pe(("i", 2))
-        hid_sort("V", 0, 1)
-        unit_pe(("i", 3))
+        sort(("i", 3))
+        full("tok", 1, 1)
+        dw4(1, 0)
+        unit_quant(("i", 1))
+        full("hid", 0, 0)
         unit_quant(("i", 2))
-        neg("hid", 0, 1)
+        unit_pe(("i", 3))
         hid_sort("V", 1, 0)
         unit_quant(("i", 3))
-        quant_a("hid", 0, 1)
-        quant_b("hid", 0, 1)
         dw4(1, 1)
-        neg("hid", 1, 0)
+        full("hid", 1, 0)
         for it in range(4):
             dx(0, it, 0, it)
-        hid_sort("V", 1, 1)
-        quant_a("hid", 1, 0)
-        quant_b("hid", 1, 0)
+        hid_sort("S", 0, 1, 2, 4)
+        hid_sort("V", 0, 1, 0, 2)
+        hid_sort("V", 1, 1, 0, 2)
+        neg("hid", 0, 1)
+        hid_sort("S", 1, 1, 2, 4)
+        quant_a("hid", 0, 1)
         neg("hid", 1, 1)
-        for it in range(4):
-            dx(1, it, 0, 4 + it)
-        quant_a("hid", 1, 1)
-        quant_b("hid", 1, 1)
+        quant_b("hid", 0, 1)
+        quant("hid", 1, 1)
         for it in range(4):
             dx(0, it, 1)
-            dx_out("SVSV"[it], 0, it)
+            dx_out("SSVS"[it], 0, it)
+        for it in range(4):
+            dx(1, it, 0, 4 + it)
         for it in range(4):
             dx(1, it, 1)
-            dx_out("SVSV"[it], 1, it)
+            dx_out("VSVS"[it], 1, it)

@@ -156,21 +156,24 @@ def tile_spectralattention_v_kernel(tc, x, w0, wout, zr, grad_out, out_0, out_1)
             dst = S["uvals", key][:, c * 1024 : (c + 1) * 1024].bitcast(F32).rearrange("p (m u) -> p m u", u=2)
             copy(eng, dst, S["ubank", key, c][:].rearrange("p (u m) -> p m u", u=2))
 
-        def unit_quant(key):
-            op = operand("u_%s%d" % key, 512)
-            quantize(op, E4M3, 0, S["uvals", key][:])
-            S["uop", key] = op
+        def unit_quant(key, lo=0, hi=2):
+            if lo == 0:
+                S["uop", key] = operand("u_%s%d" % key, 512)
+            quantize(S["uop", key], E4M3, lo * 256, S["uvals", key][:, lo * 1024 : hi * 1024])
 
-        def dh(g, t, parts=(0, 1)):
+        def dh_pass(g, t, c, part):
             if ("wop", g, t) in S:
                 op, r_first, i_first = S["wop", g, t]
             else:
                 op, r_first, i_first = S["uop", ("vw"[g], t // 2)], (t % 2) * P, 256 + (t % 2) * P
-            for c in parts:
-                bank = acc_bank()
-                mx(bank, op, r_first, g_op, 512 * c, True, False)
-                mx(bank, op, i_first, g_op, 512 * (c + 1), False, True)
-                S["dh", g, t, c] = bank
+            if part == 0:
+                S["dh", g, t, c] = acc_bank()
+            mx(S["dh", g, t, c], op, (r_first, i_first)[part], g_op, 512 * (c + part), part == 0, part == 1)
+
+        def dh(g, t):
+            for c in range(2):
+                for part in range(2):
+                    dh_pass(g, t, c, part)
 
         def dz_tile(g):
             if ("dz", g) not in S:
@@ -308,10 +311,10 @@ def tile_spectralattention_v_kernel(tc, x, w0, wout, zr, grad_out, out_0, out_1)
         for t in range(2, 4):
             direct_turn(t)
             direct_out(t)
-        quantize(g_op, E5M2, 0, g_vals[:, 0:2048])
         unit_quant(("v", 0))
-        quantize(g_op, E5M2, 512, g_vals[:, 2048:4096])
+        quantize(g_op, E5M2, 0, g_vals[:, 0:2048])
         negate(g_vals[:, 4096:6144], g_vals[:, 0:2048])
+        quantize(g_op, E5M2, 512, g_vals[:, 2048:4096])
         direct_quant(2)
         quantize(g_op, E5M2, 1024, g_vals[:, 4096:6144])
 
@@ -325,8 +328,10 @@ def tile_spectralattention_v_kernel(tc, x, w0, wout, zr, grad_out, out_0, out_1)
             quant(kind, g, k)
 
         sort(("w", 0), "VS")
-        dh(0, 0)
-        dh(0, 1)
+        for c in range(2):
+            for part in range(2):
+                for t in range(2):
+                    dh_pass(0, t, c, part)
         direct_quant(3)
         dz(0, 0)
         dz(0, 1)
@@ -362,13 +367,13 @@ def tile_spectralattention_v_kernel(tc, x, w0, wout, zr, grad_out, out_0, out_1)
         unit_pe(("i", 0))
         sort(("i", 1))
         unit_quant(("x", 1))
-        dw_run([(0, 0, 0), (0, 0, 1), (0, 1, 0), (0, 1, 1)], "SSSV")
+        dw_run([(0, 0, 0), (0, 0, 1), (0, 1, 0), (0, 1, 1)], "SSSS")
         tok_pe(1, 0)
         tok_pe(1, 1)
         sort(("i", 2))
         unit_quant(("i", 0))
         hid_sort("V", 0, 0)
-        dw_run([(0, 0, 2), (0, 0, 3), (0, 1, 2), (0, 1, 3)], "SSSV")
+        dw_run([(0, 0, 2), (0, 0, 3), (0, 1, 2), (0, 1, 3)], "SSSS")
         full("tok", 1, 0)
         unit_pe(("i", 1))
         unit_pe(("i", 2))
@@ -380,9 +385,10 @@ def tile_spectralattention_v_kernel(tc, x, w0, wout, zr, grad_out, out_0, out_1)
         unit_quant(("i", 2))
         unit_pe(("i", 3))
         hid_sort("V", 1, 0)
-        unit_quant(("i", 3))
         dw4(1, 1)
-        full("hid", 1, 0)
+        neg("hid", 1, 0)
+        unit_quant(("i", 3))
+        quant("hid", 1, 0)
         for it in range(4):
             dx(0, it, 0, it)
         hid_sort("S", 0, 1, 2, 4)

@@ -12,13 +12,13 @@ E5M2 = mybir.dt.float8_e5m2_x4
 ALU = mybir.AluOpType
 
 P = 128
-CIN, HID, COUT, TOK = 512, 1024, 512, 512
-NTP = 4
-NVALS = 4
-NRES = 8
-NPRE = 3
-NUV = 3
+BANK = 512
+HALF = 256
+TRIPLE = 3 * HALF
+TURN_BANKS = 4
 FLOPS = 3 * 4 * 2 * 512 * 512 * 1024
+
+VECTOR, SCALAR = "V", "S"
 
 
 def tile_spectralattention_v_kernel(tc, x, w0, wout, zr, grad_out, out_0, out_1):
@@ -29,8 +29,8 @@ def tile_spectralattention_v_kernel(tc, x, w0, wout, zr, grad_out, out_0, out_1)
         psum = ctx.enter_context(tc.psum_pool(name="psum", bufs=1))
         ctx.enter_context(tc.manual_schedule())
 
-        def copy(eng, out, in_):
-            if eng == "V":
+        def copy(engine, out, in_):
+            if engine == VECTOR:
                 nc.vector.tensor_copy(out=out, in_=in_)
             else:
                 nc.scalar.copy(out=out, in_=in_)
@@ -44,19 +44,21 @@ def tile_spectralattention_v_kernel(tc, x, w0, wout, zr, grad_out, out_0, out_1)
             nc.sync.dma_start(out=view, in_=src)
             return dst
 
-        def operand(name, width):
-            codes = keep.tile([P, width], U32, name=name + "_codes", align_bytes=64)
-            scales = keep.tile([P, width], U8, name=name + "_scales", align_bytes=64)
+        def operand(name, words):
+            codes = keep.tile([P, words], U32, name=name + "_codes", align_bytes=256)
+            scales = keep.tile([P, words], U8, name=name + "_scales", align_bytes=256)
             return codes, scales
 
         def quantize(op, fmt, first, values):
-            width = values.shape[1] // 4
-            cols = slice(first, first + width)
+            cols = slice(first, first + values.shape[1] // 4)
             nc.vector.quantize_mx(out=op[0][:, cols].bitcast(fmt), scales=op[1][:, cols], in_=values)
+
+        def negate(out, in_):
+            nc.vector.tensor_scalar(out=out, in0=in_, scalar1=-1.0, scalar2=None, op0=ALU.mult)
 
         def mx(bank, weights, w_first, moving, m_first, start, stop):
             w_cols = slice(w_first, w_first + P)
-            m_cols = slice(m_first, m_first + 512)
+            m_cols = slice(m_first, m_first + BANK)
             nc.tensor.matmul_mx(
                 out=bank[:],
                 lhsT=weights[0][:, w_cols].bitcast(E4M3),
@@ -67,22 +69,33 @@ def tile_spectralattention_v_kernel(tc, x, w0, wout, zr, grad_out, out_0, out_1)
                 stop=stop,
             )
 
-        turns = {"tp": 0, "acc": 0}
-
         def bank_at(n):
-            bank = psum.tile([P, 512], F32, name="bank%d" % n, tag="bank%d" % n)
+            bank = psum.tile([P, BANK], F32, name="bank%d" % n, tag="bank%d" % n)
             return bank
 
-        def tp_bank():
-            turns["tp"] = turns["tp"] + 1
-            return bank_at((turns["tp"] - 1) % NTP)
+        taken = {"turn": 0, "sum": 0}
 
-        def acc_bank():
-            turns["acc"] = turns["acc"] + 1
-            return bank_at(NTP + (turns["acc"] - 1) % (8 - NTP))
+        def next_bank(role):
+            n = taken[role] % TURN_BANKS
+            taken[role] = taken[role] + 1
+            return bank_at(n if role == "turn" else TURN_BANKS + n)
 
-        def negate(out, in_):
-            nc.vector.tensor_scalar(out=out, in0=in_, scalar1=-1.0, scalar2=None, op0=ALU.mult)
+        def turn(words):
+            bank = next_bank("turn")
+            for s in range(4):
+                nc.tensor.transpose(bank[:, s * P : (s + 1) * P], words[s], ident[:])
+            return bank
+
+        def word_runs(tile, firsts):
+            return [tile[:, first : first + 2 * P].bitcast(F32) for first in firsts]
+
+        def store(engine, dst, view, src, pieces=1):
+            res = work.tile([P, BANK], F32, name="res", tag="res", bufs=6)
+            ordered = view(res[:])
+            rows, width = ordered.shape[1] // pieces, BANK // pieces
+            for n in range(pieces):
+                copy(engine, ordered[:, n * rows : (n + 1) * rows], src[:, n * rows : (n + 1) * rows])
+                nc.sync.dma_start(out=dst[:, n * width : (n + 1) * width], in_=res[:, n * width : (n + 1) * width])
 
         ident = keep.tile([P, P], F32, name="ident")
         make_identity(nc, ident[:])
@@ -95,316 +108,295 @@ def tile_spectralattention_v_kernel(tc, x, w0, wout, zr, grad_out, out_0, out_1)
         dx_v = out_0.rearrange("b i y z c -> (b i) (y z c)")
         dw_v = out_1.rearrange("i h c -> i (h c)")
 
-        S = {}
+        def triple_values(name):
+            vals = work.tile([P, 8 * TRIPLE], BF16, name=name, tag="vals", bufs=4, align_bytes=64)
+            return vals
 
-        g_vals = work.tile([P, 6144], BF16, name="g_vals", tag="vals", bufs=NVALS, align_bytes=64)
-        g_op = operand("g", 1536)
+        g_vals = triple_values("g_vals")
+        g_op = operand("g", 3 * BANK)
+        g_part = [g_vals[:, n * 4 * BANK : (n + 1) * 4 * BANK] for n in range(3)]
 
-        def g_sort(eng, half, lo=0, hi=2):
-            dst = g_vals[:, 0:4096].rearrange("p (c h y i t) -> p h c y t i", c=2, h=2, i=4, t=4)[:, half]
-            src = S["g", half][:].rearrange("p (t y i c) -> p c y t i", t=4, i=4, c=2)
-            copy(eng, dst[:, lo:hi], src[:, lo:hi])
+        def g_sort(engine, half, c_from, c_to):
+            dst = g_vals[:, : 8 * BANK].rearrange("p (c h y i t) -> p h c y t i", c=2, h=2, i=4, t=4)[:, half]
+            src = g_raw[half][:].rearrange("p (t y i c) -> p c y t i", t=4, i=4, c=2)
+            copy(engine, dst[:, c_from:c_to], src[:, c_from:c_to])
 
-        def direct_turn(t):
-            words = S["wout0", t][:].bitcast(F32)
-            bank = tp_bank()
-            for s in range(4):
-                nc.tensor.transpose(bank[:, s * P : (s + 1) * P], words[:, s:512:4], ident[:])
-            S["dbank", t] = bank
+        def g_quantize(n):
+            quantize(g_op, E5M2, n * BANK, g_part[n])
 
-        def direct_out(t):
-            vals = work.tile([P, 1024], BF16, name="dvals", tag="dvals", bufs=2, align_bytes=64)
+        raw, sorted_pair, pair_vals, pair_op = {}, {}, {}, {}
+
+        def sort(key, engines=VECTOR):
+            pre = work.tile([P, 4 * BANK], BF16, name="pre", tag="pre", bufs=3)
+            if key[0] == "x":
+                src = raw[key][:].rearrange("p (b u j c) -> p c u b j", u=2, j=16, c=2)
+                dst = pre[:].rearrange("p (c u b j) -> p c u b j", c=2, u=2, j=16)
+            else:
+                src = raw[key][:].rearrange("p (q u e c) -> p c u q e", u=2, e=2, c=2)
+                dst = pre[:].rearrange("p (c u q e) -> p c u q e", c=2, u=2, e=2)
+            if len(engines) == 2:
+                for c in range(2):
+                    copy(engines[c], dst[:, c], src[:, c])
+            else:
+                copy(engines, dst, src)
+            sorted_pair[key] = pre
+
+        def turn_pair(key):
+            for c in range(2):
+                bank = turn(word_runs(sorted_pair[key], [c * 2 * BANK + s * 2 * P for s in range(4)]))
+                if c == 0:
+                    vals = work.tile([P, 4 * BANK], BF16, name="uvals", tag="uvals", bufs=3, align_bytes=64)
+                    pair_vals[key] = vals
+                dst = pair_vals[key][:, c * 2 * BANK : (c + 1) * 2 * BANK].bitcast(F32)
+                copy(SCALAR, dst.rearrange("p (m u) -> p m u", u=2), bank[:].rearrange("p (u m) -> p m u", u=2))
+
+        def quantize_pair(key):
+            pair_op[key] = operand("pair_%s%d" % key, BANK)
+            quantize(pair_op[key], E4M3, 0, pair_vals[key][:])
+
+        def pair_columns(key, a):
+            return pair_op[key], (a * P, HALF + a * P)
+
+        single_vals, single_op = {}, {}
+
+        def turn_single(t):
+            words = raw["single", t][:].bitcast(F32)
+            bank = turn([words[:, s:BANK:4] for s in range(4)])
+            vals = work.tile([P, 2 * BANK], BF16, name="dvals", tag="dvals", bufs=2, align_bytes=64)
             nc.scalar.copy(
                 out=vals[:].rearrange("p (c m s) -> p c m s", c=2, s=4),
-                in_=S["dbank", t][:].bitcast(BF16).rearrange("p (s m c) -> p c m s", s=4, c=2),
+                in_=bank[:].bitcast(BF16).rearrange("p (s m c) -> p c m s", s=4, c=2),
             )
-            S["dvals", t] = vals
+            single_vals[t] = vals
 
-        def direct_quant(t):
-            op = operand("wd%d" % t, 256)
-            quantize(op, E4M3, 0, S["dvals", t][:])
-            S["wop", 0, t] = (op, 0, P)
+        def quantize_single(t):
+            single_op[t] = operand("single%d" % t, HALF)
+            quantize(single_op[t], E4M3, 0, single_vals[t][:])
 
-        def unit_sort(engs, key, src, tokens):
-            pre = work.tile([P, 2048], BF16, name="pre", tag="pre", bufs=NPRE)
-            if tokens:
-                a = src.rearrange("p (b u j c) -> p c u b j", u=2, j=16, c=2)
-                o = pre[:].rearrange("p (c u b j) -> p c u b j", c=2, u=2, j=16)
-            else:
-                a = src.rearrange("p (q u e c) -> p c u q e", u=2, e=2, c=2)
-                o = pre[:].rearrange("p (c u q e) -> p c u q e", c=2, u=2, e=2)
-            if len(engs) == 2:
-                for c in range(2):
-                    copy(engs[c], o[:, c], a[:, c])
-            else:
-                copy(engs, o, a)
-            S["pre", key] = pre
-
-        def unit_turn(key, c):
-            bank = tp_bank()
-            for s in range(4):
-                first = c * 1024 + s * 256
-                nc.tensor.transpose(
-                    bank[:, s * P : (s + 1) * P], S["pre", key][:, first : first + 256].bitcast(F32), ident[:]
-                )
-            S["ubank", key, c] = bank
-
-        def unit_out(eng, key, c):
-            if c == 0:
-                vals = work.tile([P, 2048], BF16, name="uvals", tag="uvals", bufs=NUV, align_bytes=64)
-                S["uvals", key] = vals
-            dst = S["uvals", key][:, c * 1024 : (c + 1) * 1024].bitcast(F32).rearrange("p (m u) -> p m u", u=2)
-            copy(eng, dst, S["ubank", key, c][:].rearrange("p (u m) -> p m u", u=2))
-
-        def unit_quant(key, lo=0, hi=2):
-            if lo == 0:
-                S["uop", key] = operand("u_%s%d" % key, 512)
-            quantize(S["uop", key], E4M3, lo * 256, S["uvals", key][:, lo * 1024 : hi * 1024])
+        dh_bank, dz_tile = {}, {}
 
         def dh_pass(g, t, c, part):
-            if ("wop", g, t) in S:
-                op, r_first, i_first = S["wop", g, t]
+            if g == 0 and t >= 2:
+                op, firsts = single_op[t], (0, P)
             else:
-                op, r_first, i_first = S["uop", ("vw"[g], t // 2)], (t % 2) * P, 256 + (t % 2) * P
+                op, firsts = pair_columns(("wout", 2 * g + t // 2), t % 2)
             if part == 0:
-                S["dh", g, t, c] = acc_bank()
-            mx(S["dh", g, t, c], op, (r_first, i_first)[part], g_op, 512 * (c + part), part == 0, part == 1)
+                dh_bank[g, t, c] = next_bank("sum")
+            mx(dh_bank[g, t, c], op, firsts[part], g_op, (c + part) * BANK, part == 0, part == 1)
 
         def dh(g, t):
             for c in range(2):
                 for part in range(2):
                     dh_pass(g, t, c, part)
 
-        def dz_tile(g):
-            if ("dz", g) not in S:
-                dz = keep.tile([P, 4096], BF16, name="dz%d" % g)
-                S["dz", g] = dz
-            return S["dz", g]
-
-        def dz_re(g, t):
-            saved = S["zr", g, t // 2][:, (t % 2) * 512 : (t % 2 + 1) * 512]
+        def dz(g, t):
+            if t == 0:
+                dz_tile[g] = keep.tile([P, 8 * BANK], BF16, name="dz%d" % g)
+            first = t * 2 * BANK
+            saved = zr_raw[g, t // 2][:, (t % 2) * BANK : (t % 2 + 1) * BANK]
             saved = saved.rearrange("p (b u j) -> p u b j", u=2, j=16)
-            bank = S["dh", g, t, 0][:].rearrange("p (b u j) -> p u b j", u=2, j=16)
-            dst = dz_tile(g)[:, t * 1024 : t * 1024 + 512].rearrange("p (u b j) -> p u b j", u=2, j=16)
+            dhr = dh_bank[g, t, 0][:].rearrange("p (b u j) -> p u b j", u=2, j=16)
+            dzr = dz_tile[g][:, first : first + BANK].rearrange("p (u b j) -> p u b j", u=2, j=16)
             for u in range(2):
                 nc.vector.scalar_tensor_tensor(
-                    out=dst[:, u], in0=saved[:, u], scalar=0.0, in1=bank[:, u], op0=ALU.is_gt, op1=ALU.mult
+                    out=dzr[:, u], in0=saved[:, u], scalar=0.0, in1=dhr[:, u], op0=ALU.is_gt, op1=ALU.mult
                 )
+            dzi = dz_tile[g][:, first + BANK : first + 2 * BANK].rearrange("p (u b j) -> p b u j", u=2, j=16)
+            copy(SCALAR, dzi, dh_bank[g, t, 1][:].rearrange("p (b u j) -> p b u j", u=2, j=16))
 
-        def dz_im(eng, g, t):
-            dst = dz_tile(g)[:, t * 1024 + 512 : (t + 1) * 1024].rearrange("p (u b j) -> p b u j", u=2, j=16)
-            copy(eng, dst, S["dh", g, t, 1][:].rearrange("p (b u j) -> p b u j", u=2, j=16))
+        dz_vals, dz_op = {}, {}
 
-        def tok_turn(g, a, c):
-            bank = tp_bank()
-            for s in range(4):
-                first = (2 * a + s // 2) * 1024 + c * 512 + (s % 2) * 256
-                nc.tensor.transpose(
-                    bank[:, s * P : (s + 1) * P], S["dz", g][:, first : first + 256].bitcast(F32), ident[:]
-                )
-            S["tbank", g, a, c] = bank
+        def way_values(way, g):
+            if (way, g) not in dz_vals:
+                dz_vals[way, g] = triple_values(way)
+                dz_op[way, g] = operand("%s%d" % (way, g), 2 * TRIPLE)
+            return dz_vals[way, g]
 
-        def vals_tile(kind, g):
-            if (kind, g) not in S:
-                vals = work.tile([P, 6144], BF16, name=kind, tag="vals", bufs=NVALS, align_bytes=64)
-                S[kind, g] = vals
-                S[kind + "op", g] = operand("%s%d" % (kind, g), 1536)
-            return S[kind, g]
+        def turn_dz(g, a):
+            for c in range(2):
+                firsts = [(2 * a + s // 2) * 2 * BANK + c * BANK + (s % 2) * HALF for s in range(4)]
+                bank = turn(word_runs(dz_tile[g], firsts))
+                dst = way_values("tok", g)[:].bitcast(F32)
+                dst = dst.rearrange("p (k c m a s) -> p c a k m s", k=2, c=3, a=2, s=4)
+                copy(SCALAR, dst[:, c, a], bank[:].rearrange("p (s k m) -> p k m s", s=4, k=2))
 
-        def tok_out(eng, g, a, c):
-            dst = vals_tile("tok", g)[:].bitcast(F32).rearrange("p (k c m a s) -> p c a k m s", k=2, c=3, a=2, s=4)
-            copy(eng, dst[:, c, a], S["tbank", g, a, c][:].rearrange("p (s k m) -> p k m s", s=4, k=2))
+        def interleave_dz(engine, g, k, v_from=0, v_to=4):
+            dst = way_values("hid", g)[:, k * 4 * TRIPLE : k * 4 * TRIPLE + 8 * HALF]
+            dst = dst.rearrange("p (v y i t) -> p v y t i", v=4, i=4, t=4)
+            src = dz_tile[g][:].rearrange("p (t v k y i) -> p k v y t i", t=4, v=4, k=2, i=4)[:, k]
+            copy(engine, dst[:, v_from:v_to], src[:, v_from:v_to])
 
-        def hid_sort(eng, g, k, lo=0, hi=4):
-            dst = vals_tile("hid", g)[:, k * 3072 : k * 3072 + 2048].rearrange("p (v y i t) -> p v y t i", v=4, i=4, t=4)
-            src = S["dz", g][:].rearrange("p (t v k y i) -> p k v y t i", t=4, v=4, k=2, i=4)[:, k]
-            copy(eng, dst[:, lo:hi], src[:, lo:hi])
+        def negate_dz(way, g, k):
+            first = k * 4 * TRIPLE
+            vals = dz_vals[way, g]
+            negate(vals[:, first + 8 * HALF : first + 12 * HALF], vals[:, first : first + 4 * HALF])
 
-        def neg(kind, g, k):
-            vals = S[kind, g]
-            negate(vals[:, k * 3072 + 2048 : (k + 1) * 3072], vals[:, k * 3072 : k * 3072 + 1024])
+        def quantize_dz(way, g, k):
+            first = k * 4 * TRIPLE
+            vals = dz_vals[way, g]
+            quantize(dz_op[way, g], E5M2, k * TRIPLE, vals[:, first : first + 8 * HALF])
+            quantize(dz_op[way, g], E5M2, k * TRIPLE + 2 * HALF, vals[:, first + 8 * HALF : first + 12 * HALF])
 
-        def quant_a(kind, g, k):
-            quantize(S[kind + "op", g], E5M2, k * 768, S[kind, g][:, k * 3072 : k * 3072 + 2048])
+        def finish_dz(way, g, k):
+            negate_dz(way, g, k)
+            quantize_dz(way, g, k)
 
-        def quant_b(kind, g, k):
-            quantize(S[kind + "op", g], E5M2, k * 768 + 512, S[kind, g][:, k * 3072 + 2048 : (k + 1) * 3072])
-
-        def dw(g, k, it):
-            op, first = S["uop", ("x", it // 2)], (it % 2) * P
-            bank = acc_bank()
-            mx(bank, op, first, S["tokop", g], k * 768, True, False)
-            mx(bank, op, 256 + first, S["tokop", g], k * 768 + 256, False, True)
-            S["dw", g, k, it] = bank
-
-        def dw_out(eng, g, k, it):
-            res = work.tile([P, 512], F32, name="res", tag="res", bufs=NRES)
-            copy(eng, res[:].rearrange("p (h c) -> p h c", c=2), S["dw", g, k, it][:].rearrange("p (c h) -> p h c", c=2))
-            first = g * 1024 + k * 512
-            nc.sync.dma_start(out=dw_v[it * P : (it + 1) * P, first : first + 512], in_=res[:])
-
-        def dx(k, it, g, n=None):
-            op = S["uop", ("i", it)]
-            if g == 0:
-                S["dx", k, it] = acc_bank() if n is None else bank_at(n)
-            bank = S["dx", k, it]
-            mx(bank, op, g * P, S["hidop", g], k * 768, g == 0, False)
-            mx(bank, op, 256 + g * P, S["hidop", g], k * 768 + 256, False, g == 1)
-
-        def dx_out(eng, k, it):
-            res = work.tile([P, 512], F32, name="res", tag="res", bufs=NRES)
-            copy(
-                eng,
-                res[:].rearrange("p (b u j c) -> p b u j c", u=2, j=16, c=2),
-                S["dx", k, it][:].rearrange("p (c u b j) -> p b u j c", c=2, u=2, j=16),
+        def dw(g, k, it, bank):
+            op, firsts = pair_columns(("x", it // 2), it % 2)
+            for part in range(2):
+                mx(bank, op, firsts[part], dz_op["tok", g], k * TRIPLE + part * HALF, part == 0, part == 1)
+            first = (2 * g + k) * BANK
+            store(
+                SCALAR,
+                dw_v[it * P : (it + 1) * P, first : first + BANK],
+                lambda res: res.rearrange("p (h c) -> p h c", c=2),
+                bank[:].rearrange("p (c h) -> p h c", c=2),
             )
-            nc.sync.dma_start(out=dx_v[it * P : (it + 1) * P, k * 512 : (k + 1) * 512], in_=res[:])
 
+        dx_bank = {}
 
-        def unit_pe(key, engs="SS"):
-            for c in range(2):
-                unit_turn(key, c)
-                unit_out(engs[c], key, c)
+        def dx(k, it, g):
+            op, firsts = pair_columns(("w0", it), g)
+            for part in range(2):
+                start, stop = g == 0 and part == 0, g == 1 and part == 1
+                mx(dx_bank[k, it], op, firsts[part], dz_op["hid", g], k * TRIPLE + part * HALF, start, stop)
 
-        def sort(key, engs="V"):
-            unit_sort(engs, key, S[key][:], key[0] == "x")
+        def dx_store(engine, k, it, pieces=1):
+            store(
+                engine,
+                dx_v[it * P : (it + 1) * P, k * BANK : (k + 1) * BANK],
+                lambda res: res.rearrange("p (b u j c) -> p b u j c", u=2, j=16, c=2),
+                dx_bank[k, it][:].rearrange("p (c u b j) -> p b u j c", c=2, u=2, j=16),
+                pieces,
+            )
 
-        def tok_pe(g, a, engs="SS"):
-            for c in range(2):
-                tok_turn(g, a, c)
-                tok_out(engs[c], g, a, c)
-
-        def dz(g, t):
-            dz_re(g, t)
-            dz_im("S", g, t)
-
-        def dw4(g, k, engs="SSSS"):
-            for it in range(4):
-                dw(g, k, it)
-                dw_out(engs[it], g, k, it)
-
-        def quant(kind, g, k):
-            quant_a(kind, g, k)
-            quant_b(kind, g, k)
-
-        S["v", 0] = load("wout00", wout_v[0, :, 0:2, :], BF16)
-        S["g", 0] = load("g0", g_v[:, :, 0:512], BF16)
-        S["g", 1] = load("g1", g_v[:, :, 512:1024], BF16)
+        g_raw, zr_raw = {}, {}
+        raw["wout", 0] = load("wout00", wout_v[0, :, 0:2, :], BF16)
+        for half in range(2):
+            g_raw[half] = load("g%d" % half, g_v[:, :, half * BANK : (half + 1) * BANK], BF16)
         for t in range(2, 4):
-            S["wout0", t] = load("wout0%d" % t, wout_v[0, :, t, :], BF16)
-        S["zr", 0, 0] = load("zr00", zr_v[0, :, 0:2, :], F32)
-        S["w", 0] = load("wout10", wout_v[1, :, 0:2, :], BF16)
-        S["zr", 0, 1] = load("zr01", zr_v[0, :, 2:4, :], F32)
-        S["w", 1] = load("wout11", wout_v[1, :, 2:4, :], BF16)
-        S["x", 0] = load("x0", x_v[:, 0:2, :], BF16)
-        S["zr", 1, 0] = load("zr10", zr_v[1, :, 0:2, :], F32)
-        S["x", 1] = load("x1", x_v[:, 2:4, :], BF16)
-        S["zr", 1, 1] = load("zr11", zr_v[1, :, 2:4, :], F32)
+            raw["single", t] = load("wout0%d" % t, wout_v[0, :, t, :], BF16)
+        for a in range(2):
+            zr_raw[0, a] = load("zr0%d" % a, zr_v[0, :, 2 * a : 2 * a + 2, :], F32)
+            raw["wout", 2 + a] = load("wout1%d" % a, wout_v[1, :, 2 * a : 2 * a + 2, :], BF16)
+        for a in range(2):
+            raw["x", a] = load("x%d" % a, x_v[:, 2 * a : 2 * a + 2, :], BF16)
+            zr_raw[1, a] = load("zr1%d" % a, zr_v[1, :, 2 * a : 2 * a + 2, :], F32)
         for it in range(4):
-            S["i", it] = load("w0%d" % it, w0_v[it], BF16)
+            raw["w0", it] = load("w0%d" % it, w0_v[it], BF16)
 
-        sort(("v", 0), "VV")
-        unit_pe(("v", 0))
-        g_sort("V", 0)
-        g_sort("V", 1, 0, 1)
-        g_sort("S", 1, 1, 2)
+        sort(("wout", 0), VECTOR + VECTOR)
+        turn_pair(("wout", 0))
+        g_sort(VECTOR, 0, 0, 2)
+        g_sort(VECTOR, 1, 0, 1)
+        g_sort(SCALAR, 1, 1, 2)
         for t in range(2, 4):
-            direct_turn(t)
-            direct_out(t)
-        unit_quant(("v", 0))
-        quantize(g_op, E5M2, 0, g_vals[:, 0:2048])
-        negate(g_vals[:, 4096:6144], g_vals[:, 0:2048])
-        quantize(g_op, E5M2, 512, g_vals[:, 2048:4096])
-        direct_quant(2)
-        quantize(g_op, E5M2, 1024, g_vals[:, 4096:6144])
+            turn_single(t)
+        quantize_pair(("wout", 0))
+        g_quantize(0)
+        negate(g_part[2], g_part[0])
+        g_quantize(1)
+        quantize_single(2)
+        g_quantize(2)
+        sort(("wout", 2), VECTOR + SCALAR)
 
-        def dw_run(pairs, engs):
-            for n, (g, k, it) in enumerate(pairs):
-                dw(g, k, it)
-                dw_out(engs[n], g, k, it)
 
-        def full(kind, g, k):
-            neg(kind, g, k)
-            quant(kind, g, k)
-
-        sort(("w", 0), "VS")
         for c in range(2):
             for part in range(2):
                 for t in range(2):
                     dh_pass(0, t, c, part)
-        direct_quant(3)
+        quantize_single(3)
         dz(0, 0)
         dz(0, 1)
-        unit_pe(("w", 0))
-        sort(("w", 1))
+        turn_pair(("wout", 2))
+        sort(("wout", 3))
+
         dh(0, 2)
         dh(0, 3)
-        sort(("x", 0))
-        unit_quant(("w", 0))
+        sort(("x", 0), VECTOR + SCALAR)
+        quantize_pair(("wout", 2))
         dz(0, 2)
         dz(0, 3)
-        unit_pe(("w", 1))
-        unit_pe(("x", 0))
+        turn_pair(("wout", 3))
+        turn_pair(("x", 0))
         sort(("x", 1))
+
         dh(1, 0)
         dh(1, 1)
-        unit_quant(("w", 1))
+        quantize_pair(("wout", 3))
         dz(1, 0)
         dz(1, 1)
-        tok_pe(0, 0)
-        tok_pe(0, 1)
-        sort(("i", 0))
-        unit_quant(("x", 0))
+        turn_dz(0, 0)
+        turn_dz(0, 1)
+        sort(("w0", 0))
+        quantize_pair(("x", 0))
+
         dh(1, 2)
         dh(1, 3)
         dz(1, 2)
-        neg("tok", 0, 0)
-        neg("tok", 0, 1)
-        quant("tok", 0, 0)
+        negate_dz("tok", 0, 0)
+        negate_dz("tok", 0, 1)
+        quantize_dz("tok", 0, 0)
         dz(1, 3)
-        quant("tok", 0, 1)
-        unit_pe(("x", 1))
-        unit_pe(("i", 0))
-        sort(("i", 1))
-        unit_quant(("x", 1))
-        dw_run([(0, 0, 0), (0, 0, 1), (0, 1, 0), (0, 1, 1)], "SSSS")
-        tok_pe(1, 0)
-        tok_pe(1, 1)
-        sort(("i", 2))
-        unit_quant(("i", 0))
-        hid_sort("V", 0, 0)
-        dw_run([(0, 0, 2), (0, 0, 3), (0, 1, 2), (0, 1, 3)], "SSSS")
-        full("tok", 1, 0)
-        unit_pe(("i", 1))
-        unit_pe(("i", 2))
-        sort(("i", 3))
-        full("tok", 1, 1)
-        dw4(1, 0)
-        unit_quant(("i", 1))
-        full("hid", 0, 0)
-        unit_quant(("i", 2))
-        unit_pe(("i", 3))
-        hid_sort("V", 1, 0)
-        dw4(1, 1)
-        neg("hid", 1, 0)
-        unit_quant(("i", 3))
-        quant("hid", 1, 0)
+        quantize_dz("tok", 0, 1)
+        turn_pair(("x", 1))
+        turn_pair(("w0", 0))
+        sort(("w0", 1))
+        quantize_pair(("x", 1))
+
+        for k in range(2):
+            for it in range(2):
+                dw(0, k, it, next_bank("sum"))
+        turn_dz(1, 0)
+        turn_dz(1, 1)
+        sort(("w0", 2))
+        quantize_pair(("w0", 0))
+        interleave_dz(VECTOR, 0, 0)
+
+        for k in range(2):
+            for it in range(2, 4):
+                dw(0, k, it, next_bank("sum"))
+        finish_dz("tok", 1, 0)
+        turn_pair(("w0", 1))
+        turn_pair(("w0", 2))
+        sort(("w0", 3))
+        finish_dz("tok", 1, 1)
+
         for it in range(4):
-            dx(0, it, 0, it)
-        hid_sort("S", 0, 1, 2, 4)
-        hid_sort("V", 0, 1, 0, 2)
-        hid_sort("V", 1, 1, 0, 2)
-        neg("hid", 0, 1)
-        hid_sort("S", 1, 1, 2, 4)
-        quant_a("hid", 0, 1)
-        neg("hid", 1, 1)
-        quant_b("hid", 0, 1)
-        quant("hid", 1, 1)
+            dw(1, 0, it, next_bank("sum"))
+        quantize_pair(("w0", 1))
+        finish_dz("hid", 0, 0)
+        quantize_pair(("w0", 2))
+        turn_pair(("w0", 3))
+        interleave_dz(VECTOR, 1, 0)
+
+        older, newer = (0, 1, 4, 5), (6, 7, 2, 3)
+        for it in range(4):
+            dw(1, 1, it, bank_at(older[it]))
+        negate_dz("hid", 1, 0)
+        quantize_pair(("w0", 3))
+        quantize_dz("hid", 1, 0)
+
+        for it in range(4):
+            dx_bank[0, it] = bank_at(newer[it])
+            dx(0, it, 0)
+        interleave_dz(VECTOR, 0, 1)
+        interleave_dz(SCALAR, 1, 1, 0, 2)
+        interleave_dz(SCALAR, 1, 1, 2, 4)
+        finish_dz("hid", 0, 1)
+        finish_dz("hid", 1, 1)
         for it in range(4):
             dx(0, it, 1)
-            dx_out("SSVS"[it], 0, it)
-        for it in range(4):
-            dx(1, it, 0, 4 + it)
-        for it in range(4):
+            dx_store(VECTOR if it == 2 else SCALAR, 0, it)
+
+        for it in range(2):
+            dx_bank[1, it] = bank_at(older[it])
+            dx(1, it, 0)
+        for it in range(2):
             dx(1, it, 1)
-            dx_out("VSVS"[it], 1, it)
+            dx_store((VECTOR, SCALAR)[it], 1, it)
+        for it in range(2, 4):
+            dx_bank[1, it] = bank_at(older[it])
+            dx(1, it, 0)
+            dx(1, it, 1)
+            dx_store((SCALAR, VECTOR)[it - 2], 1, it, pieces=it - 1)

from contextlib import ExitStack

import concourse.mybir as mybir
from concourse.masks import make_identity

F32 = mybir.dt.float32
BF16 = mybir.dt.bfloat16
U32 = mybir.dt.uint32
U8 = mybir.dt.uint8
E4M3 = mybir.dt.float8_e4m3fn_x4
E5M2 = mybir.dt.float8_e5m2_x4
ALU = mybir.AluOpType

P = 128
BANK = 512
HALF = 256
TRIPLE = 3 * HALF
TURN_BANKS = 4
FLOPS = 3 * 4 * 2 * 512 * 512 * 1024

VECTOR, SCALAR = "V", "S"


def tile_spectralattention_v_kernel(tc, x, w0, wout, zr, grad_out, out_0, out_1):
    nc = tc.nc
    with ExitStack() as ctx:
        keep = ctx.enter_context(tc.tile_pool(name="keep", bufs=1))
        work = ctx.enter_context(tc.tile_pool(name="work", bufs=2))
        psum = ctx.enter_context(tc.psum_pool(name="psum", bufs=1))
        ctx.enter_context(tc.manual_schedule())

        def copy(engine, out, in_):
            if engine == VECTOR:
                nc.vector.tensor_copy(out=out, in_=in_)
            else:
                nc.scalar.copy(out=out, in_=in_)

        def load(name, src, dtype):
            width = src.shape[1] if len(src.shape) == 2 else src.shape[1] * src.shape[2]
            dst = keep.tile([P, width], dtype, name=name)
            view = dst[:]
            if len(src.shape) == 3:
                view = view.rearrange("p (a w) -> p a w", a=src.shape[1])
            nc.sync.dma_start(out=view, in_=src)
            return dst

        def operand(name, words):
            codes = keep.tile([P, words], U32, name=name + "_codes", align_bytes=256)
            scales = keep.tile([P, words], U8, name=name + "_scales", align_bytes=256)
            return codes, scales

        def quantize(op, fmt, first, values):
            cols = slice(first, first + values.shape[1] // 4)
            nc.vector.quantize_mx(out=op[0][:, cols].bitcast(fmt), scales=op[1][:, cols], in_=values)

        def negate(out, in_):
            nc.vector.tensor_scalar(out=out, in0=in_, scalar1=-1.0, scalar2=None, op0=ALU.mult)

        def mx(bank, weights, w_first, moving, m_first, start, stop):
            w_cols = slice(w_first, w_first + P)
            m_cols = slice(m_first, m_first + BANK)
            nc.tensor.matmul_mx(
                out=bank[:],
                lhsT=weights[0][:, w_cols].bitcast(E4M3),
                lhsT_scale=weights[1][:, w_cols],
                rhs=moving[0][:, m_cols].bitcast(E5M2),
                rhs_scale=moving[1][:, m_cols],
                start=start,
                stop=stop,
            )

        def bank_at(n):
            bank = psum.tile([P, BANK], F32, name="bank%d" % n, tag="bank%d" % n)
            return bank

        taken = {"turn": 0, "sum": 0}

        def next_bank(role):
            n = taken[role] % TURN_BANKS
            taken[role] = taken[role] + 1
            return bank_at(n if role == "turn" else TURN_BANKS + n)

        def turn(words):
            bank = next_bank("turn")
            for s in range(4):
                nc.tensor.transpose(bank[:, s * P : (s + 1) * P], words[s], ident[:])
            return bank

        def word_runs(tile, firsts):
            return [tile[:, first : first + 2 * P].bitcast(F32) for first in firsts]

        def store(engine, dst, view, src, pieces=1):
            res = work.tile([P, BANK], F32, name="res", tag="res", bufs=6)
            ordered = view(res[:])
            rows, width = ordered.shape[1] // pieces, BANK // pieces
            for n in range(pieces):
                copy(engine, ordered[:, n * rows : (n + 1) * rows], src[:, n * rows : (n + 1) * rows])
                nc.sync.dma_start(out=dst[:, n * width : (n + 1) * width], in_=res[:, n * width : (n + 1) * width])

        ident = keep.tile([P, P], F32, name="ident")
        make_identity(nc, ident[:])

        wout_v = wout.rearrange("(g m t) o c -> g m t (o c)", g=2, t=4)
        zr_v = zr.rearrange("b (g m t) y z -> (b g) m t (y z)", g=2, t=4)
        g_v = grad_out.rearrange("b (q t) y z c -> (b q) t (y z c)", t=4)
        x_v = x.rearrange("b (a m) y z c -> m (b a) (y z c)", m=P)
        w0_v = w0.rearrange("(a m) h c -> a m (h c)", m=P)
        dx_v = out_0.rearrange("b i y z c -> (b i) (y z c)")
        dw_v = out_1.rearrange("i h c -> i (h c)")

        def triple_values(name):
            vals = work.tile([P, 8 * TRIPLE], BF16, name=name, tag="vals", bufs=4, align_bytes=64)
            return vals

        g_vals = triple_values("g_vals")
        g_op = operand("g", 3 * BANK)
        g_part = [g_vals[:, n * 4 * BANK : (n + 1) * 4 * BANK] for n in range(3)]

        def g_sort(engine, half, c_from, c_to):
            dst = g_vals[:, : 8 * BANK].rearrange("p (c h y i t) -> p h c y t i", c=2, h=2, i=4, t=4)[:, half]
            src = g_raw[half][:].rearrange("p (t y i c) -> p c y t i", t=4, i=4, c=2)
            copy(engine, dst[:, c_from:c_to], src[:, c_from:c_to])

        def g_quantize(n):
            quantize(g_op, E5M2, n * BANK, g_part[n])

        raw, sorted_pair, pair_vals, pair_op = {}, {}, {}, {}

        def sort(key, engines=VECTOR):
            pre = work.tile([P, 4 * BANK], BF16, name="pre", tag="pre", bufs=3)
            if key[0] == "x":
                src = raw[key][:].rearrange("p (b u j c) -> p c u b j", u=2, j=16, c=2)
                dst = pre[:].rearrange("p (c u b j) -> p c u b j", c=2, u=2, j=16)
            else:
                src = raw[key][:].rearrange("p (q u e c) -> p c u q e", u=2, e=2, c=2)
                dst = pre[:].rearrange("p (c u q e) -> p c u q e", c=2, u=2, e=2)
            if len(engines) == 2:
                for c in range(2):
                    copy(engines[c], dst[:, c], src[:, c])
            else:
                copy(engines, dst, src)
            sorted_pair[key] = pre

        def turn_pair(key):
            for c in range(2):
                bank = turn(word_runs(sorted_pair[key], [c * 2 * BANK + s * 2 * P for s in range(4)]))
                if c == 0:
                    vals = work.tile([P, 4 * BANK], BF16, name="uvals", tag="uvals", bufs=3, align_bytes=64)
                    pair_vals[key] = vals
                dst = pair_vals[key][:, c * 2 * BANK : (c + 1) * 2 * BANK].bitcast(F32)
                copy(SCALAR, dst.rearrange("p (m u) -> p m u", u=2), bank[:].rearrange("p (u m) -> p m u", u=2))

        def quantize_pair(key):
            pair_op[key] = operand("pair_%s%d" % key, BANK)
            quantize(pair_op[key], E4M3, 0, pair_vals[key][:])

        def pair_columns(key, a):
            return pair_op[key], (a * P, HALF + a * P)

        single_vals, single_op = {}, {}

        def turn_single(t):
            words = raw["single", t][:].bitcast(F32)
            bank = turn([words[:, s:BANK:4] for s in range(4)])
            vals = work.tile([P, 2 * BANK], BF16, name="dvals", tag="dvals", bufs=2, align_bytes=64)
            nc.scalar.copy(
                out=vals[:].rearrange("p (c m s) -> p c m s", c=2, s=4),
                in_=bank[:].bitcast(BF16).rearrange("p (s m c) -> p c m s", s=4, c=2),
            )
            single_vals[t] = vals

        def quantize_single(t):
            single_op[t] = operand("single%d" % t, HALF)
            quantize(single_op[t], E4M3, 0, single_vals[t][:])

        dh_bank, dz_tile = {}, {}

        def dh_pass(g, t, c, part):
            if g == 0 and t >= 2:
                op, firsts = single_op[t], (0, P)
            else:
                op, firsts = pair_columns(("wout", 2 * g + t // 2), t % 2)
            if part == 0:
                dh_bank[g, t, c] = next_bank("sum")
            mx(dh_bank[g, t, c], op, firsts[part], g_op, (c + part) * BANK, part == 0, part == 1)

        def dh(g, t):
            for c in range(2):
                for part in range(2):
                    dh_pass(g, t, c, part)

        def dz(g, t):
            if t == 0:
                dz_tile[g] = keep.tile([P, 8 * BANK], BF16, name="dz%d" % g)
            first = t * 2 * BANK
            saved = zr_raw[g, t // 2][:, (t % 2) * BANK : (t % 2 + 1) * BANK]
            saved = saved.rearrange("p (b u j) -> p u b j", u=2, j=16)
            dhr = dh_bank[g, t, 0][:].rearrange("p (b u j) -> p u b j", u=2, j=16)
            dzr = dz_tile[g][:, first : first + BANK].rearrange("p (u b j) -> p u b j", u=2, j=16)
            for u in range(2):
                nc.vector.scalar_tensor_tensor(
                    out=dzr[:, u], in0=saved[:, u], scalar=0.0, in1=dhr[:, u], op0=ALU.is_gt, op1=ALU.mult
                )
            dzi = dz_tile[g][:, first + BANK : first + 2 * BANK].rearrange("p (u b j) -> p b u j", u=2, j=16)
            copy(SCALAR, dzi, dh_bank[g, t, 1][:].rearrange("p (b u j) -> p b u j", u=2, j=16))

        dz_vals, dz_op = {}, {}

        def way_values(way, g):
            if (way, g) not in dz_vals:
                dz_vals[way, g] = triple_values(way)
                dz_op[way, g] = operand("%s%d" % (way, g), 2 * TRIPLE)
            return dz_vals[way, g]

        def turn_dz(g, a):
            for c in range(2):
                firsts = [(2 * a + s // 2) * 2 * BANK + c * BANK + (s % 2) * HALF for s in range(4)]
                bank = turn(word_runs(dz_tile[g], firsts))
                dst = way_values("tok", g)[:].bitcast(F32)
                dst = dst.rearrange("p (k c m a s) -> p c a k m s", k=2, c=3, a=2, s=4)
                copy(SCALAR, dst[:, c, a], bank[:].rearrange("p (s k m) -> p k m s", s=4, k=2))

        def interleave_dz(engine, g, k, v_from=0, v_to=4):
            dst = way_values("hid", g)[:, k * 4 * TRIPLE : k * 4 * TRIPLE + 8 * HALF]
            dst = dst.rearrange("p (v y i t) -> p v y t i", v=4, i=4, t=4)
            src = dz_tile[g][:].rearrange("p (t v k y i) -> p k v y t i", t=4, v=4, k=2, i=4)[:, k]
            copy(engine, dst[:, v_from:v_to], src[:, v_from:v_to])

        def negate_dz(way, g, k):
            first = k * 4 * TRIPLE
            vals = dz_vals[way, g]
            negate(vals[:, first + 8 * HALF : first + 12 * HALF], vals[:, first : first + 4 * HALF])

        def quantize_dz(way, g, k):
            first = k * 4 * TRIPLE
            vals = dz_vals[way, g]
            quantize(dz_op[way, g], E5M2, k * TRIPLE, vals[:, first : first + 8 * HALF])
            quantize(dz_op[way, g], E5M2, k * TRIPLE + 2 * HALF, vals[:, first + 8 * HALF : first + 12 * HALF])

        def finish_dz(way, g, k):
            negate_dz(way, g, k)
            quantize_dz(way, g, k)

        def dw(g, k, it, bank):
            op, firsts = pair_columns(("x", it // 2), it % 2)
            for part in range(2):
                mx(bank, op, firsts[part], dz_op["tok", g], k * TRIPLE + part * HALF, part == 0, part == 1)
            first = (2 * g + k) * BANK
            store(
                SCALAR,
                dw_v[it * P : (it + 1) * P, first : first + BANK],
                lambda res: res.rearrange("p (h c) -> p h c", c=2),
                bank[:].rearrange("p (c h) -> p h c", c=2),
            )

        dx_bank = {}

        def dx(k, it, g):
            op, firsts = pair_columns(("w0", it), g)
            for part in range(2):
                start, stop = g == 0 and part == 0, g == 1 and part == 1
                mx(dx_bank[k, it], op, firsts[part], dz_op["hid", g], k * TRIPLE + part * HALF, start, stop)

        def dx_store(engine, k, it, pieces=1):
            store(
                engine,
                dx_v[it * P : (it + 1) * P, k * BANK : (k + 1) * BANK],
                lambda res: res.rearrange("p (b u j c) -> p b u j c", u=2, j=16, c=2),
                dx_bank[k, it][:].rearrange("p (c u b j) -> p b u j c", c=2, u=2, j=16),
                pieces,
            )

        g_raw, zr_raw = {}, {}
        raw["wout", 0] = load("wout00", wout_v[0, :, 0:2, :], BF16)
        for half in range(2):
            g_raw[half] = load("g%d" % half, g_v[:, :, half * BANK : (half + 1) * BANK], BF16)
        for t in range(2, 4):
            raw["single", t] = load("wout0%d" % t, wout_v[0, :, t, :], BF16)
        for a in range(2):
            zr_raw[0, a] = load("zr0%d" % a, zr_v[0, :, 2 * a : 2 * a + 2, :], F32)
            raw["wout", 2 + a] = load("wout1%d" % a, wout_v[1, :, 2 * a : 2 * a + 2, :], BF16)
        for a in range(2):
            raw["x", a] = load("x%d" % a, x_v[:, 2 * a : 2 * a + 2, :], BF16)
            zr_raw[1, a] = load("zr1%d" % a, zr_v[1, :, 2 * a : 2 * a + 2, :], F32)
        for it in range(4):
            raw["w0", it] = load("w0%d" % it, w0_v[it], BF16)

        sort(("wout", 0), VECTOR + VECTOR)
        turn_pair(("wout", 0))
        g_sort(VECTOR, 0, 0, 2)
        g_sort(VECTOR, 1, 0, 1)
        g_sort(SCALAR, 1, 1, 2)
        for t in range(2, 4):
            turn_single(t)
        quantize_pair(("wout", 0))
        g_quantize(0)
        negate(g_part[2], g_part[0])
        g_quantize(1)
        quantize_single(2)
        g_quantize(2)
        sort(("wout", 2), VECTOR + SCALAR)


        for c in range(2):
            for part in range(2):
                for t in range(2):
                    dh_pass(0, t, c, part)
        quantize_single(3)
        dz(0, 0)
        dz(0, 1)
        turn_pair(("wout", 2))
        sort(("wout", 3))

        dh(0, 2)
        dh(0, 3)
        sort(("x", 0), VECTOR + SCALAR)
        quantize_pair(("wout", 2))
        dz(0, 2)
        dz(0, 3)
        turn_pair(("wout", 3))
        turn_pair(("x", 0))
        sort(("x", 1))

        dh(1, 0)
        dh(1, 1)
        quantize_pair(("wout", 3))
        dz(1, 0)
        dz(1, 1)
        turn_dz(0, 0)
        turn_dz(0, 1)
        sort(("w0", 0))
        quantize_pair(("x", 0))

        dh(1, 2)
        dh(1, 3)
        dz(1, 2)
        negate_dz("tok", 0, 0)
        negate_dz("tok", 0, 1)
        quantize_dz("tok", 0, 0)
        dz(1, 3)
        quantize_dz("tok", 0, 1)
        turn_pair(("x", 1))
        turn_pair(("w0", 0))
        sort(("w0", 1))
        quantize_pair(("x", 1))

        for k in range(2):
            for it in range(2):
                dw(0, k, it, next_bank("sum"))
        turn_dz(1, 0)
        turn_dz(1, 1)
        sort(("w0", 2))
        quantize_pair(("w0", 0))
        interleave_dz(VECTOR, 0, 0)

        for k in range(2):
            for it in range(2, 4):
                dw(0, k, it, next_bank("sum"))
        finish_dz("tok", 1, 0)
        turn_pair(("w0", 1))
        turn_pair(("w0", 2))
        sort(("w0", 3))
        finish_dz("tok", 1, 1)

        for it in range(4):
            dw(1, 0, it, next_bank("sum"))
        quantize_pair(("w0", 1))
        finish_dz("hid", 0, 0)
        quantize_pair(("w0", 2))
        turn_pair(("w0", 3))
        interleave_dz(VECTOR, 1, 0)

        older, newer = (0, 1, 4, 5), (6, 7, 2, 3)
        for it in range(4):
            dw(1, 1, it, bank_at(older[it]))
        negate_dz("hid", 1, 0)
        quantize_pair(("w0", 3))
        quantize_dz("hid", 1, 0)

        for it in range(4):
            dx_bank[0, it] = bank_at(newer[it])
            dx(0, it, 0)
        interleave_dz(VECTOR, 0, 1)
        interleave_dz(SCALAR, 1, 1, 0, 2)
        interleave_dz(SCALAR, 1, 1, 2, 4)
        finish_dz("hid", 0, 1)
        finish_dz("hid", 1, 1)
        for it in range(4):
            dx(0, it, 1)
            dx_store(VECTOR if it == 2 else SCALAR, 0, it)

        for it in range(2):
            dx_bank[1, it] = bank_at(older[it])
            dx(1, it, 0)
        for it in range(2):
            dx(1, it, 1)
            dx_store((VECTOR, SCALAR)[it], 1, it)
        for it in range(2, 4):
            dx_bank[1, it] = bank_at(older[it])
            dx(1, it, 0)
            dx(1, it, 1)
            dx_store((SCALAR, VECTOR)[it - 2], 1, it, pieces=it - 1)
